import numpy as np
import ml_dtypes


def mxq(x, axis, fmt="e4m3"):
    dtype, down = {"e4m3": (ml_dtypes.float8_e4m3fn, 7), "e5m2": (ml_dtypes.float8_e5m2, 14)}[fmt]
    v = np.moveaxis(np.asarray(x, np.float32).astype(ml_dtypes.bfloat16).astype(np.float64), axis, -1)
    blocks = v.reshape(v.shape[:-1] + (-1, 32))
    amax = np.abs(blocks).max(-1, keepdims=True)
    byte = np.maximum(np.where(amax > 0, np.frexp(amax)[1] - 1 + 127, 0) - down, 1)
    scale = np.exp2(byte - 127.0)
    codes = (blocks / scale).astype(np.float32).astype(dtype).astype(np.float64)
    return np.moveaxis((codes * scale).reshape(v.shape), -1, axis)


WIDE = False


def mx_kscale(k):
    if not WIDE:
        return np.ones(k)
    levels = np.array([10, -10, 5, -5, 0])
    if k % 512:
        return np.exp2(np.random.permutation(np.resize(levels, k // 32))).repeat(32)
    a = np.empty((k // 512, 16))
    for p in range(k // 512):
        a[p, :8] = np.random.permutation(np.resize(levels, 8))
        for g in range(8):
            far = levels[np.abs(levels - a[p, g]) >= 10]
            a[p, g + 8] = far[np.random.randint(len(far))]
    return np.exp2(a.ravel()).repeat(32)


BF16 = ml_dtypes.bfloat16


def bf(x):
    return np.asarray(x, np.float32).astype(BF16)


def f64(x):
    return np.asarray(x).astype(np.float64)


B, C, C4, H, W, R = 1, 512, 512, 64, 64, 4
ND = 2 * R + 1
GAIN = 1.2
QS = GAIN * C4 ** 0.25
BS = 0.3 * QS


def setup_inputs():
    s, t = mx_kscale(C), mx_kscale(C4)
    return {"x": bf(np.random.standard_normal((B, C, H, W)) * s[None, :, None, None]),
            "y": bf(np.random.standard_normal((B, C, H, W)) * s[None, :, None, None]),
            "query_w": bf(np.random.standard_normal((C4, C)) * QS / np.sqrt(C) * t[:, None] / s[None, :]),
            "query_b": bf(np.random.standard_normal(C4) * BS * t),
            "key_w": bf(np.random.standard_normal((C4, C)) * QS / np.sqrt(C) / t[:, None] / s[None, :]),
            "key_b": bf(np.random.standard_normal(C4) * BS / t)}


def reference(x, y, query_w, query_b, key_w, key_b):
    yq = mxq(f64(y).reshape(B, C, H * W), 1, "e4m3")
    xq = mxq(f64(x).reshape(B, C, H * W), 1, "e4m3")
    q = (mxq(f64(query_w), 1, "e4m3") @ yq) + f64(query_b)[None, :, None]
    k = (mxq(f64(key_w), 1, "e4m3") @ xq) + f64(key_b)[None, :, None]
    qq = mxq(q, 1, "e4m3").reshape(B, C4, H, W).transpose(0, 2, 3, 1)
    kq = mxq(k, 1, "e4m3").reshape(B, C4, H, W).transpose(0, 2, 1, 3)
    corr = np.zeros((B, H, W, ND * ND))
    for di in range(ND):
        oi = di - R
        i0, i1 = max(0, -oi), min(H, H - oi)
        sc = qq[:, i0:i1] @ kq[:, i0 + oi:i1 + oi]
        for dj in range(ND):
            oj = dj - R
            w0, w1 = max(0, -oj), min(W, W - oj)
            corr[:, i0:i1, w0:w1, di * ND + dj] = np.diagonal(sc, offset=oj, axis1=2, axis2=3)
    corr = corr / C4
    e = np.exp(corr - corr.max(-1, keepdims=True))
    return e / e.sum(-1, keepdims=True)

@@ -1,0 +1,345 @@
+from contextlib import ExitStack
+
+import concourse.mybir as mybir
+from concourse.masks import make_identity
+
+F32 = mybir.dt.float32
+BF16 = mybir.dt.bfloat16
+U32 = mybir.dt.uint32
+U8 = mybir.dt.uint8
+I32 = mybir.dt.int32
+FP8X4 = mybir.dt.float8_e4m3fn_x4
+
+P = 128
+PACK = 4
+CHANNELS = P * PACK
+HEIGHT = 64
+WIDTH = 64
+REACH = 4
+SHIFTS = 2 * REACH + 1
+CELLS = SHIFTS * SHIFTS
+
+BLOCK_ROWS = 8
+BLOCKS = HEIGHT // BLOCK_ROWS
+BLOCK_PIXELS = BLOCK_ROWS * WIDTH
+PAIR_PIXELS = 2 * WIDTH
+PAIRS = BLOCK_ROWS // 2
+
+PATCH_COLS = P // BLOCK_ROWS
+PATCHES = WIDTH // PATCH_COLS
+WINDOW_ROWS = BLOCK_ROWS + 2 * REACH
+WINDOW_COLS = PATCH_COLS + 2 * REACH
+K_BLOCKS = BLOCKS + 1
+K_MARGIN = 8
+K_COLS = WIDTH + 2 * K_MARGIN
+K_BLOCK_WORDS = K_COLS * BLOCK_ROWS
+STREAM_COLS = 32
+STREAM_SKIP = K_MARGIN - REACH
+
+PARK_RUN = SHIFTS * WINDOW_COLS
+PARK_STEP = PARK_RUN + 1
+PARK_READ = (SHIFTS - 1) * WINDOW_COLS + SHIFTS
+PARK_ROW = WIDTH * PARK_STEP
+PARK_BLOCK = BLOCK_ROWS * PARK_ROW
+PARK_SLOTS = 2
+OUT_FLOATS = HEIGHT * WIDTH * CELLS
+OUT_BLOCK = BLOCK_PIXELS * CELLS
+PARK_START = OUT_FLOATS - PARK_SLOTS * PARK_BLOCK
+
+FLOPS = 2 * 2 * CHANNELS * CHANNELS * HEIGHT * WIDTH + 2 * CHANNELS * CELLS * HEIGHT * WIDTH
+
+
+def park_base(block):
+    return PARK_START + (block % PARK_SLOTS) * PARK_BLOCK
+
+
+def last_block_parked_on(block):
+    first, end = block * OUT_BLOCK, (block + 1) * OUT_BLOCK
+    users = [b for b in range(BLOCKS) if park_base(b) < end and first < park_base(b) + PARK_BLOCK]
+    return max(users) if users else -1
+
+
+def tile_local_module_pa_t_kernel(tc, x, y, query_w, query_b, key_w, key_b, out):
+    nc = tc.nc
+    with ExitStack() as ctx:
+        keep = ctx.enter_context(tc.tile_pool(name="keep", bufs=1))
+        weight_stage = ctx.enter_context(tc.tile_pool(name="weight_stage", bufs=2))
+        raw_pool = ctx.enter_context(tc.tile_pool(name="raw", bufs=BLOCKS))
+        stage = ctx.enter_context(tc.tile_pool(name="stage", bufs=2))
+        k_stage = ctx.enter_context(tc.tile_pool(name="k_stage", bufs=3))
+        small = ctx.enter_context(tc.tile_pool(name="small", bufs=2))
+        project_psum = ctx.enter_context(tc.psum_pool(name="project_psum", bufs=4))
+        corr_psum = ctx.enter_context(tc.psum_pool(name="corr_psum", bufs=4))
+
+        q_codes = keep.tile([P, BLOCKS * BLOCK_PIXELS], U32, align_bytes=64)
+        q_scales = keep.tile([P, BLOCKS * BLOCK_PIXELS], U8, align_bytes=64)
+        k_codes = keep.tile([P, K_BLOCKS * K_BLOCK_WORDS], U32, align_bytes=64)
+        k_scales = keep.tile([P, K_BLOCKS * K_BLOCK_WORDS], U8, align_bytes=64)
+        result = keep.tile([P, BLOCKS, PAIRS, CELLS], F32)
+        identity = keep.tile([P, P], F32)
+        make_identity(nc, identity[:])
+
+        margin_words = K_MARGIN * BLOCK_ROWS
+        code_blocks = k_codes[:].bitcast(I32).rearrange("p (b w) -> p b w", w=K_BLOCK_WORDS)
+        scale_blocks = k_scales[:].bitcast(I32).rearrange("p (b w) -> p b w", w=K_BLOCK_WORDS // 4)
+        nc.vector.memset(code_blocks[:, :, 0:margin_words], 0)
+        nc.vector.memset(code_blocks[:, :, K_BLOCK_WORDS - margin_words :], 0)
+        nc.vector.memset(scale_blocks[:, :, 0 : margin_words // 4], 0)
+        nc.vector.memset(scale_blocks[:, :, (K_BLOCK_WORDS - margin_words) // 4 :], 0)
+
+        def load_weight(w):
+            rows = weight_stage.tile([P, PACK, CHANNELS], BF16, name="w_rows")
+            nc.sync.dma_start(out=rows[:], in_=w.rearrange("(p m) c -> p m c", m=PACK))
+            return rows
+
+        def quantise_weight(rows, name):
+            grouped = weight_stage.tile([P, CHANNELS, PACK], BF16, name="w_grouped", align_bytes=64)
+            for m in range(PACK):
+                flipped = corr_psum.tile([P, 2, P], F32, name="flipped", tag="corr_bank")
+                words = rows[:, m, :].bitcast(F32)
+                for u in range(2):
+                    nc.tensor.transpose(flipped[:, u, :], words[:, u::2], identity[:])
+                nc.vector.tensor_copy(
+                    out=grouped[:, m * P : (m + 1) * P, :].rearrange("p o j -> p (o j)").bitcast(F32)
+                    .rearrange("p (o u) -> p o u", u=2),
+                    in_=flipped[:].rearrange("p u o -> p o u"),
+                )
+            codes = keep.tile([P, CHANNELS], U32, name=name + "_codes", align_bytes=64)
+            scales = keep.tile([P, CHANNELS], U8, name=name + "_scales", align_bytes=64)
+            nc.vector.quantize_mx(
+                out=codes[:].bitcast(FP8X4), scales=scales[:], in_=grouped[:].rearrange("p o j -> p (o j)")
+            )
+            return codes, scales
+
+        def load_bias(b, name):
+            bias = keep.tile([P, PACK], BF16, name=name)
+            nc.sync.dma_start(out=bias[:], in_=b.rearrange("(p t) -> p t", t=PACK))
+            return bias
+
+        def load_input(image, block, name):
+            planes = image.rearrange("b (p j) h w -> p (b j) (h w)", j=PACK)
+            raw = raw_pool.tile([P, PACK, BLOCK_PIXELS], BF16, name=name + "_raw")
+            nc.sync.dma_start(out=raw[:], in_=planes[:, :, block * BLOCK_PIXELS : (block + 1) * BLOCK_PIXELS])
+            return raw
+
+        def regroup_input(raw, name):
+            grouped = stage.tile([P, BLOCK_PIXELS, PACK], BF16, name=name + "_grouped", align_bytes=64)
+            nc.scalar.copy(
+                out=grouped[:].rearrange("p (c i) j -> p c j i", i=4),
+                in_=raw[:].rearrange("p j (c i) -> p c j i", i=4),
+            )
+            return grouped
+
+        def quantise_input(grouped, name):
+            codes = stage.tile([P, BLOCK_PIXELS], U32, name=name + "_codes", align_bytes=64)
+            scales = stage.tile([P, BLOCK_PIXELS], U8, name=name + "_scales", align_bytes=64)
+            nc.vector.quantize_mx(
+                out=codes[:].bitcast(FP8X4), scales=scales[:], in_=grouped[:].rearrange("p w j -> p (w j)")
+            )
+            return codes, scales
+
+        def project(pixels, pair, weight, bias, target):
+            codes, scales = pixels
+            w_codes, w_scales = weight
+            cols = slice(pair * PAIR_PIXELS, (pair + 1) * PAIR_PIXELS)
+            bank = project_psum.tile([P, PACK, PAIR_PIXELS], F32, name="bank")
+            for t in range(PACK):
+                channels = slice(t * P, (t + 1) * P)
+                nc.tensor.matmul_mx(
+                    out=bank[:, t, :],
+                    lhsT=w_codes[:, channels].bitcast(FP8X4),
+                    lhsT_scale=w_scales[:, channels],
+                    rhs=codes[:, cols].bitcast(FP8X4),
+                    rhs_scale=scales[:, cols],
+                    start=True,
+                    stop=True,
+                )
+            nc.vector.tensor_tensor(
+                out=target,
+                in0=bank[:].rearrange("p t (i j) -> p j i t", i=2),
+                in1=bias[:].unsqueeze(1).unsqueeze(1).to_broadcast([P, WIDTH, 2, PACK]),
+                op=mybir.AluOpType.add,
+            )
+
+        def new_k_block(k_block):
+            grouped = k_stage.tile([P, WIDTH, BLOCK_ROWS, PACK], BF16, name="k_grouped", align_bytes=64)
+            if k_block == 0:
+                nc.vector.memset(grouped[:, :, 0:REACH, :], 0.0)
+            if k_block == K_BLOCKS - 1:
+                nc.vector.memset(grouped[:, :, REACH:, :], 0.0)
+            return grouped
+
+        def quantise_k_block(grouped, k_block):
+            first = k_block * K_BLOCK_WORDS + margin_words
+            nc.vector.quantize_mx(
+                out=k_codes[:, first : first + BLOCK_PIXELS].bitcast(FP8X4),
+                scales=k_scales[:, first : first + BLOCK_PIXELS],
+                in_=grouped[:].rearrange("p j r t -> p (j r t)"),
+            )
+
+        out_flat = out.rearrange("b h w d -> (b h w d)")
+        out_pixels = out.rearrange("b h w d -> (b h w) d")
+
+        def correlate(block):
+            products = stage.tile([P, PATCHES, WINDOW_ROWS * WINDOW_COLS], F32, name="products")
+            for patch in range(PATCHES):
+                q_cols = slice(block * BLOCK_PIXELS + patch * P, block * BLOCK_PIXELS + (patch + 1) * P)
+                bank = corr_psum.tile([P, 2, STREAM_COLS * BLOCK_ROWS], F32, name="corr_bank")
+                for half in range(2):
+                    first = (block + half) * K_BLOCK_WORDS + patch * PATCH_COLS * BLOCK_ROWS
+                    k_cols = slice(first, first + STREAM_COLS * BLOCK_ROWS)
+                    nc.tensor.matmul_mx(
+                        out=bank[:, half, :],
+                        lhsT=q_codes[:, q_cols].bitcast(FP8X4),
+                        lhsT_scale=q_scales[:, q_cols],
+                        rhs=k_codes[:, k_cols].bitcast(FP8X4),
+                        rhs_scale=k_scales[:, k_cols],
+                        start=True,
+                        stop=True,
+                    )
+                nc.scalar.copy(
+                    out=products[:, patch, :].rearrange("p (h r c) -> p h r c", h=2, r=BLOCK_ROWS),
+                    in_=bank[:].rearrange("p h (c r) -> p h r c", r=BLOCK_ROWS)[
+                        :, :, :, STREAM_SKIP : STREAM_SKIP + WINDOW_COLS
+                    ],
+                )
+            for r in range(BLOCK_ROWS):
+                row_base = park_base(block) + r * PARK_ROW
+                parked = (
+                    out_flat[row_base : row_base + PARK_ROW]
+                    .rearrange("(a s) -> a s", s=PATCH_COLS * PARK_STEP)[:, 0 : PATCH_COLS * PARK_RUN]
+                    .rearrange("a (c s) -> c a s", s=PARK_RUN)
+                )
+                nc.sync.dma_start(
+                    out=parked, in_=products[r:P:BLOCK_ROWS, :, r * WINDOW_COLS : r * WINDOW_COLS + PARK_RUN]
+                )
+
+        def read_back(block):
+            windows = stage.tile([P, PAIRS, PARK_RUN], F32, name="windows")
+            base = park_base(block)
+            nc.sync.dma_start(
+                out=windows[:, :, 0:PARK_READ],
+                in_=out_flat[base : base + PARK_BLOCK].rearrange("(m p s) -> p m s", p=P, s=PARK_STEP)[
+                    :, :, 0:PARK_READ
+                ],
+            )
+            return windows
+
+        def window_cells(windows):
+            return windows[:].rearrange("p m (d c) -> p m d c", c=WINDOW_COLS)[:, :, :, 0:SHIFTS]
+
+        def softmax_shift(windows):
+            top = small.tile([P, PAIRS], F32, name="top")
+            nc.vector.tensor_reduce(
+                out=top[:], in_=window_cells(windows), axis=mybir.AxisListType.XY, op=mybir.AluOpType.max
+            )
+            shift = small.tile([P, PAIRS], F32, name="shift")
+            nc.vector.tensor_scalar_mul(out=shift[:], in0=top[:], scalar1=-1.0 / CHANNELS)
+            return shift
+
+        def softmax_powers(windows, shift):
+            powers = stage.tile([P, PAIRS, CELLS], F32, name="powers")
+            total = small.tile([P, PAIRS], F32, name="total")
+            for m in range(PAIRS):
+                nc.scalar.activation(
+                    out=powers[:, m, :].rearrange("p (d c) -> p d c", c=SHIFTS),
+                    in_=window_cells(windows)[:, m],
+                    func=mybir.ActivationFunctionType.Exp,
+                    bias=shift[:, m : m + 1],
+                    scale=1.0 / CHANNELS,
+                    accum_out=total[:, m : m + 1],
+                )
+            return powers, total
+
+        def softmax_divide(block, powers, total):
+            inverse = small.tile([P, PAIRS], F32, name="inverse")
+            nc.vector.reciprocal(out=inverse[:], in_=total[:])
+            for m in range(PAIRS):
+                nc.scalar.mul(out=result[:, block, m, :], in_=powers[:, m, :], mul=inverse[:, m : m + 1])
+
+        def store(block):
+            nc.sync.dma_start(
+                out=out_pixels[block * BLOCK_PIXELS : (block + 1) * BLOCK_PIXELS, :].rearrange(
+                    "(m p) d -> p m d", p=P
+                ),
+                in_=result[:, block],
+            )
+
+        def store_what_is_free(block):
+            for done in range(block + 1):
+                if max(done, last_block_parked_on(done)) == block:
+                    store(done)
+
+        def project_k(pixels, pair, grouped):
+            first = (2 * pair + REACH) % BLOCK_ROWS
+            project(pixels, pair, key_weight, key_bias, grouped[:, :, first : first + 2, :])
+
+        def project_q(pixels, pair, grouped):
+            project(pixels, pair, query_weight, query_bias, grouped[:, :, 2 * pair : 2 * pair + 2, :])
+
+        ctx.enter_context(tc.manual_schedule())
+        key_rows = load_weight(key_w)
+        x_raw = {0: load_input(x, 0, "x")}
+        query_rows = load_weight(query_w)
+        y_raw = {0: load_input(y, 0, "y")}
+        key_bias = load_bias(key_b, "key_bias")
+        query_bias = load_bias(query_b, "query_bias")
+        for block in range(1, BLOCKS):
+            x_raw[block] = load_input(x, block, "x")
+            y_raw[block] = load_input(y, block, "y")
+
+        key_weight = quantise_weight(key_rows, "key_w")
+        x_grouped = regroup_input(x_raw[0], "x")
+        y_grouped = regroup_input(y_raw[0], "y")
+        next_x_pixels = quantise_input(x_grouped, "x")
+        query_weight = quantise_weight(query_rows, "query_w")
+        next_y_pixels = quantise_input(y_grouped, "y")
+
+        k_grouped = new_k_block(0)
+        windows = {}
+        shift = {}
+        for step in range(BLOCKS + 3):
+            projecting = step < BLOCKS
+            preparing = step + 1 < BLOCKS
+            correlating = 0 <= step - 1 < BLOCKS
+            shifting = 0 <= step - 2 < BLOCKS
+            dividing = 0 <= step - 3
+            x_pixels, y_pixels = next_x_pixels, next_y_pixels
+            if dividing:
+                powers, total = softmax_powers(windows[step - 3], shift[step - 3])
+            if projecting:
+                project_k(x_pixels, 0, k_grouped)
+                project_k(x_pixels, 1, k_grouped)
+            if preparing:
+                x_grouped = regroup_input(x_raw[step + 1], "x")
+                y_grouped = regroup_input(y_raw[step + 1], "y")
+            if projecting:
+                q_grouped = stage.tile([P, WIDTH, BLOCK_ROWS, PACK], BF16, name="q_grouped", align_bytes=64)
+                project_q(y_pixels, 0, q_grouped)
+            if step < K_BLOCKS:
+                quantise_k_block(k_grouped, step)
+            if projecting:
+                project_q(y_pixels, 1, q_grouped)
+                project_q(y_pixels, 2, q_grouped)
+                project_q(y_pixels, 3, q_grouped)
+            if dividing:
+                softmax_divide(step - 3, powers, total)
+                store_what_is_free(step - 3)
+            if correlating:
+                correlate(step - 1)
+                windows[step - 1] = read_back(step - 1)
+            if preparing:
+                next_x_pixels = quantise_input(x_grouped, "x")
+            if projecting:
+                k_grouped = new_k_block(step + 1)
+                project_k(x_pixels, 2, k_grouped)
+                project_k(x_pixels, 3, k_grouped)
+                nc.vector.quantize_mx(
+                    out=q_codes[:, step * BLOCK_PIXELS : (step + 1) * BLOCK_PIXELS].bitcast(FP8X4),
+                    scales=q_scales[:, step * BLOCK_PIXELS : (step + 1) * BLOCK_PIXELS],
+                    in_=q_grouped[:].rearrange("p j r t -> p (j r t)"),
+                )
+            if preparing:
+                next_y_pixels = quantise_input(y_grouped, "y")
+            if shifting:
+                shift[step - 2] = softmax_shift(windows[step - 2])

@@ -38,7 +38,7 @@ STREAM_SKIP = K_MARGIN - REACH
 
 PARK_RUN = SHIFTS * WINDOW_COLS
 PARK_STEP = PARK_RUN + 1
-PARK_READ = (SHIFTS - 1) * WINDOW_COLS + SHIFTS
+PARK_READ = (PAIRS - 1) * PARK_STEP + (SHIFTS - 1) * WINDOW_COLS + SHIFTS
 PARK_ROW = WIDTH * PARK_STEP
 PARK_BLOCK = BLOCK_ROWS * PARK_ROW
 PARK_SLOTS = 2
@@ -215,18 +215,16 @@ def tile_local_module_pa_t_kernel(tc, x, y, query_w, query_b, key_w, key_b, out)
                 )
 
         def read_back(block):
-            windows = stage.tile([P, PAIRS, PARK_RUN], F32, name="windows")
+            windows = stage.tile([P, PAIRS, PARK_STEP], F32, name="windows")
             base = park_base(block)
             nc.sync.dma_start(
-                out=windows[:, :, 0:PARK_READ],
-                in_=out_flat[base : base + PARK_BLOCK].rearrange("(m p s) -> p m s", p=P, s=PARK_STEP)[
-                    :, :, 0:PARK_READ
-                ],
+                out=windows[:].rearrange("p m s -> p (m s)")[:, 0:PARK_READ],
+                in_=out_flat[base : base + PARK_BLOCK].rearrange("(p s) -> p s", p=P)[:, 0:PARK_READ],
             )
             return windows
 
         def window_cells(windows):
-            return windows[:].rearrange("p m (d c) -> p m d c", c=WINDOW_COLS)[:, :, :, 0:SHIFTS]
+            return windows[:, :, 0:PARK_RUN].rearrange("p m (d c) -> p m d c", c=WINDOW_COLS)[:, :, :, 0:SHIFTS]
 
         def softmax_shift(windows):
             top = small.tile([P, PAIRS], F32, name="top")
@@ -260,9 +258,9 @@ def tile_local_module_pa_t_kernel(tc, x, y, query_w, query_b, key_w, key_b, out)
         def store(block):
             nc.sync.dma_start(
                 out=out_pixels[block * BLOCK_PIXELS : (block + 1) * BLOCK_PIXELS, :].rearrange(
-                    "(m p) d -> p m d", p=P
+                    "(p m) d -> p (m d)", p=P
                 ),
-                in_=result[:, block],
+                in_=result[:, block].rearrange("p m d -> p (m d)"),
             )
 
         def store_what_is_free(block):

@@ -66,6 +66,7 @@ def tile_local_module_pa_t_kernel(tc, x, y, query_w, query_b, key_w, key_b, out)
         weight_stage = ctx.enter_context(tc.tile_pool(name="weight_stage", bufs=2))
         raw_pool = ctx.enter_context(tc.tile_pool(name="raw", bufs=BLOCKS))
         stage = ctx.enter_context(tc.tile_pool(name="stage", bufs=2))
+        regrouped = ctx.enter_context(tc.tile_pool(name="regrouped", bufs=1))
         k_stage = ctx.enter_context(tc.tile_pool(name="k_stage", bufs=3))
         small = ctx.enter_context(tc.tile_pool(name="small", bufs=2))
         project_psum = ctx.enter_context(tc.psum_pool(name="project_psum", bufs=4))
@@ -87,23 +88,40 @@ def tile_local_module_pa_t_kernel(tc, x, y, query_w, query_b, key_w, key_b, out)
         nc.vector.memset(scale_blocks[:, :, 0 : margin_words // 4], 0)
         nc.vector.memset(scale_blocks[:, :, (K_BLOCK_WORDS - margin_words) // 4 :], 0)
 
+        k_first = keep.tile([P, WIDTH, BLOCK_ROWS, PACK], BF16, align_bytes=64)
+        k_last = keep.tile([P, WIDTH, BLOCK_ROWS, PACK], BF16, align_bytes=64)
+        nc.vector.memset(k_first[:, :, 0:REACH, :], 0.0)
+        nc.gpsimd.memset(k_last[:, :, REACH:, :], 0.0)
+
         def load_weight(w):
             rows = weight_stage.tile([P, PACK, CHANNELS], BF16, name="w_rows")
-            nc.sync.dma_start(out=rows[:], in_=w.rearrange("(p m) c -> p m c", m=PACK))
+            for m in range(0, PACK, 2):
+                nc.sync.dma_start(
+                    out=rows[:, m : m + 2, :], in_=w.rearrange("(p m) c -> p m c", m=PACK)[:, m : m + 2, :]
+                )
             return rows
 
-        def quantise_weight(rows, name):
-            grouped = weight_stage.tile([P, CHANNELS, PACK], BF16, name="w_grouped", align_bytes=64)
+        def turn_weight(rows):
+            banks = []
             for m in range(PACK):
                 flipped = corr_psum.tile([P, 2, P], F32, name="flipped", tag="corr_bank")
                 words = rows[:, m, :].bitcast(F32)
                 for u in range(2):
                     nc.tensor.transpose(flipped[:, u, :], words[:, u::2], identity[:])
-                nc.vector.tensor_copy(
-                    out=grouped[:, m * P : (m + 1) * P, :].rearrange("p o j -> p (o j)").bitcast(F32)
-                    .rearrange("p (o u) -> p o u", u=2),
-                    in_=flipped[:].rearrange("p u o -> p o u"),
-                )
+                banks.append(flipped)
+            return banks
+
+        def new_grouped_weight():
+            return weight_stage.tile([P, CHANNELS, PACK], BF16, name="w_grouped", align_bytes=64)
+
+        def gather_weight(copy, banks, m, grouped):
+            copy(
+                out=grouped[:, m * P : (m + 1) * P, :].rearrange("p o j -> p (o j)").bitcast(F32)
+                .rearrange("p (o u) -> p o u", u=2),
+                in_=banks[m][:].rearrange("p u o -> p o u"),
+            )
+
+        def quantise_weight(grouped, name):
             codes = keep.tile([P, CHANNELS], U32, name=name + "_codes", align_bytes=64)
             scales = keep.tile([P, CHANNELS], U8, name=name + "_scales", align_bytes=64)
             nc.vector.quantize_mx(
@@ -113,7 +131,7 @@ def tile_local_module_pa_t_kernel(tc, x, y, query_w, query_b, key_w, key_b, out)
 
         def load_bias(b, name):
             bias = keep.tile([P, PACK], BF16, name=name)
-            nc.sync.dma_start(out=bias[:], in_=b.rearrange("(p t) -> p t", t=PACK))
+            nc.scalar.dma_start(out=bias[:], in_=b.rearrange("(p t) -> p t", t=PACK))
             return bias
 
         def load_input(image, block, name):
@@ -122,12 +140,27 @@ def tile_local_module_pa_t_kernel(tc, x, y, query_w, query_b, key_w, key_b, out)
             nc.sync.dma_start(out=raw[:], in_=planes[:, :, block * BLOCK_PIXELS : (block + 1) * BLOCK_PIXELS])
             return raw
 
-        def regroup_input(raw, name):
-            grouped = stage.tile([P, BLOCK_PIXELS, PACK], BF16, name=name + "_grouped", align_bytes=64)
-            nc.scalar.copy(
-                out=grouped[:].rearrange("p (c i) j -> p c j i", i=4),
-                in_=raw[:].rearrange("p j (c i) -> p c j i", i=4),
+        def new_grouped_input(name):
+            return regrouped.tile([P, BLOCK_PIXELS, PACK], BF16, name=name + "_grouped", align_bytes=64)
+
+        def gpsimd_copy(out, in_):
+            nc.gpsimd.tensor_scalar(
+                out=out, in0=in_, scalar1=1.0, scalar2=0.0, op0=mybir.AluOpType.mult, op1=mybir.AluOpType.add
             )
+
+        def regroup_columns(copy, raw, grouped, first, end):
+            if copy is gpsimd_copy:
+                copy(out=grouped[:, first:end, :], in_=raw[:, :, first:end].rearrange("p j c -> p c j"))
+            else:
+                copy(
+                    out=grouped[:, first:end, :].rearrange("p (c i) j -> p c j i", i=4),
+                    in_=raw[:, :, first:end].rearrange("p j (c i) -> p c j i", i=4),
+                )
+
+        def regroup_input(raw, name, share):
+            grouped = new_grouped_input(name)
+            regroup_columns(gpsimd_copy, raw, grouped, share, BLOCK_PIXELS)
+            regroup_columns(nc.scalar.copy, raw, grouped, 0, share)
             return grouped
 
         def quantise_input(grouped, name):
@@ -138,7 +171,7 @@ def tile_local_module_pa_t_kernel(tc, x, y, query_w, query_b, key_w, key_b, out)
             )
             return codes, scales
 
-        def project(pixels, pair, weight, bias, target):
+        def multiply(pixels, pair, weight):
             codes, scales = pixels
             w_codes, w_scales = weight
             cols = slice(pair * PAIR_PIXELS, (pair + 1) * PAIR_PIXELS)
@@ -154,6 +187,10 @@ def tile_local_module_pa_t_kernel(tc, x, y, query_w, query_b, key_w, key_b, out)
                     start=True,
                     stop=True,
                 )
+            return bank
+
+        def project(pixels, pair, weight, bias, target):
+            bank = multiply(pixels, pair, weight)
             nc.vector.tensor_tensor(
                 out=target,
                 in0=bank[:].rearrange("p t (i j) -> p j i t", i=2),
@@ -161,13 +198,24 @@ def tile_local_module_pa_t_kernel(tc, x, y, query_w, query_b, key_w, key_b, out)
                 op=mybir.AluOpType.add,
             )
 
+        def project_without_vector(pixels, pair, weight, bias, target):
+            bank = multiply(pixels, pair, weight)
+            planes = stage.tile([P, PACK, WIDTH, 2], BF16, name="planes")
+            for t in range(PACK):
+                nc.scalar.activation(
+                    out=planes[:, t],
+                    in_=bank[:, t, :].rearrange("p (i j) -> p j i", i=2),
+                    func=mybir.ActivationFunctionType.Identity,
+                    bias=bias[:, t : t + 1],
+                )
+            nc.scalar.copy(out=target, in_=planes[:].rearrange("p t j i -> p j i t"))
+
         def new_k_block(k_block):
-            grouped = k_stage.tile([P, WIDTH, BLOCK_ROWS, PACK], BF16, name="k_grouped", align_bytes=64)
             if k_block == 0:
-                nc.vector.memset(grouped[:, :, 0:REACH, :], 0.0)
+                return k_first
             if k_block == K_BLOCKS - 1:
-                nc.vector.memset(grouped[:, :, REACH:, :], 0.0)
-            return grouped
+                return k_last
+            return k_stage.tile([P, WIDTH, BLOCK_ROWS, PACK], BF16, name="k_grouped", align_bytes=64)
 
         def quantise_k_block(grouped, k_block):
             first = k_block * K_BLOCK_WORDS + margin_words
@@ -181,6 +229,7 @@ def tile_local_module_pa_t_kernel(tc, x, y, query_w, query_b, key_w, key_b, out)
         out_pixels = out.rearrange("b h w d -> (b h w) d")
 
         def correlate(block):
+            last = block == BLOCKS - 1
             products = stage.tile([P, PATCHES, WINDOW_ROWS * WINDOW_COLS], F32, name="products")
             for patch in range(PATCHES):
                 q_cols = slice(block * BLOCK_PIXELS + patch * P, block * BLOCK_PIXELS + (patch + 1) * P)
@@ -197,13 +246,17 @@ def tile_local_module_pa_t_kernel(tc, x, y, query_w, query_b, key_w, key_b, out)
                         start=True,
                         stop=True,
                     )
-                nc.scalar.copy(
-                    out=products[:, patch, :].rearrange("p (h r c) -> p h r c", h=2, r=BLOCK_ROWS),
-                    in_=bank[:].rearrange("p h (c r) -> p h r c", r=BLOCK_ROWS)[
-                        :, :, :, STREAM_SKIP : STREAM_SKIP + WINDOW_COLS
-                    ],
-                )
-            for r in range(BLOCK_ROWS):
+                target = products[:, patch, :].rearrange("p (h r c) -> p h r c", h=2, r=BLOCK_ROWS)
+                source = bank[:].rearrange("p h (c r) -> p h r c", r=BLOCK_ROWS)[
+                    :, :, :, STREAM_SKIP : STREAM_SKIP + WINDOW_COLS
+                ]
+                if last and patch % 2 == 1:
+                    nc.vector.tensor_scalar_mul(out=target, in0=source, scalar1=1.0 / CHANNELS)
+                else:
+                    nc.scalar.mul(out=target, in_=source, mul=1.0 / CHANNELS)
+            half_rows = BLOCK_ROWS // 2
+            for turn in range(BLOCK_ROWS):
+                r = turn // 2 + turn % 2 * half_rows
                 row_base = park_base(block) + r * PARK_ROW
                 parked = (
                     out_flat[row_base : row_base + PARK_ROW]
@@ -227,12 +280,14 @@ def tile_local_module_pa_t_kernel(tc, x, y, query_w, query_b, key_w, key_b, out)
             return windows[:, :, 0:PARK_RUN].rearrange("p m (d c) -> p m d c", c=WINDOW_COLS)[:, :, :, 0:SHIFTS]
 
         def softmax_shift(windows):
-            top = small.tile([P, PAIRS], F32, name="top")
-            nc.vector.tensor_reduce(
-                out=top[:], in_=window_cells(windows), axis=mybir.AxisListType.XY, op=mybir.AluOpType.max
-            )
             shift = small.tile([P, PAIRS], F32, name="shift")
-            nc.vector.tensor_scalar_mul(out=shift[:], in0=top[:], scalar1=-1.0 / CHANNELS)
+            nc.vector.tensor_reduce(
+                out=shift[:],
+                in_=window_cells(windows),
+                axis=mybir.AxisListType.XY,
+                op=mybir.AluOpType.max,
+                negate=True,
+            )
             return shift
 
         def softmax_powers(windows, shift):
@@ -244,7 +299,6 @@ def tile_local_module_pa_t_kernel(tc, x, y, query_w, query_b, key_w, key_b, out)
                     in_=window_cells(windows)[:, m],
                     func=mybir.ActivationFunctionType.Exp,
                     bias=shift[:, m : m + 1],
-                    scale=1.0 / CHANNELS,
                     accum_out=total[:, m : m + 1],
                 )
             return powers, total
@@ -263,9 +317,9 @@ def tile_local_module_pa_t_kernel(tc, x, y, query_w, query_b, key_w, key_b, out)
                 in_=result[:, block].rearrange("p m d -> p (m d)"),
             )
 
-        def store_what_is_free(block):
-            for done in range(block + 1):
-                if max(done, last_block_parked_on(done)) == block:
+        def store_what_is_free(step):
+            for done in range(BLOCKS):
+                if max(done + 3, last_block_parked_on(done) + 2) == step:
                     store(done)
 
         def project_k(pixels, pair, grouped):
@@ -276,22 +330,35 @@ def tile_local_module_pa_t_kernel(tc, x, y, query_w, query_b, key_w, key_b, out)
             project(pixels, pair, query_weight, query_bias, grouped[:, :, 2 * pair : 2 * pair + 2, :])
 
         ctx.enter_context(tc.manual_schedule())
-        key_rows = load_weight(key_w)
-        x_raw = {0: load_input(x, 0, "x")}
-        query_rows = load_weight(query_w)
-        y_raw = {0: load_input(y, 0, "y")}
         key_bias = load_bias(key_b, "key_bias")
         query_bias = load_bias(query_b, "query_bias")
+        x_raw = {0: load_input(x, 0, "x")}
+        key_rows = load_weight(key_w)
+        query_rows = load_weight(query_w)
+        y_raw = {0: load_input(y, 0, "y")}
         for block in range(1, BLOCKS):
             x_raw[block] = load_input(x, block, "x")
             y_raw[block] = load_input(y, block, "y")
 
-        key_weight = quantise_weight(key_rows, "key_w")
-        x_grouped = regroup_input(x_raw[0], "x")
-        y_grouped = regroup_input(y_raw[0], "y")
+        half = BLOCK_PIXELS // 2
+        x_grouped = new_grouped_input("x")
+        regroup_columns(nc.scalar.copy, x_raw[0], x_grouped, 0, half)
+        regroup_columns(nc.vector.tensor_copy, x_raw[0], x_grouped, half, BLOCK_PIXELS)
+        key_banks = turn_weight(key_rows)
+        key_grouped = new_grouped_weight()
+        gather_weight(nc.vector.tensor_copy, key_banks, 0, key_grouped)
+        gather_weight(nc.vector.tensor_copy, key_banks, 1, key_grouped)
+        gather_weight(nc.scalar.copy, key_banks, 2, key_grouped)
+        gather_weight(nc.scalar.copy, key_banks, 3, key_grouped)
         next_x_pixels = quantise_input(x_grouped, "x")
-        query_weight = quantise_weight(query_rows, "query_w")
-        next_y_pixels = quantise_input(y_grouped, "y")
+        key_weight = quantise_weight(key_grouped, "key_w")
+        query_banks = turn_weight(query_rows)
+        query_grouped = new_grouped_weight()
+        for m in range(PACK):
+            gather_weight(nc.scalar.copy, query_banks, m, query_grouped)
+        y_grouped = new_grouped_input("y")
+        y_share = BLOCK_PIXELS * 3 // 4
+        regroup_columns(nc.scalar.copy, y_raw[0], y_grouped, 0, y_share)
 
         k_grouped = new_k_block(0)
         windows = {}
@@ -302,30 +369,37 @@ def tile_local_module_pa_t_kernel(tc, x, y, query_w, query_b, key_w, key_b, out)
             correlating = 0 <= step - 1 < BLOCKS
             shifting = 0 <= step - 2 < BLOCKS
             dividing = 0 <= step - 3
-            x_pixels, y_pixels = next_x_pixels, next_y_pixels
+            x_pixels = next_x_pixels
+            if correlating and not projecting:
+                correlate(step - 1)
+                windows[step - 1] = read_back(step - 1)
             if dividing:
                 powers, total = softmax_powers(windows[step - 3], shift[step - 3])
             if projecting:
                 project_k(x_pixels, 0, k_grouped)
                 project_k(x_pixels, 1, k_grouped)
+            if step == 0:
+                query_weight = quantise_weight(query_grouped, "query_w")
+                regroup_columns(nc.vector.tensor_copy, y_raw[0], y_grouped, y_share, BLOCK_PIXELS)
+                next_y_pixels = quantise_input(y_grouped, "y")
+            y_pixels = next_y_pixels
             if preparing:
-                x_grouped = regroup_input(x_raw[step + 1], "x")
-                y_grouped = regroup_input(y_raw[step + 1], "y")
+                x_grouped = regroup_input(x_raw[step + 1], "x", BLOCK_PIXELS * 3 // 4)
             if projecting:
                 q_grouped = stage.tile([P, WIDTH, BLOCK_ROWS, PACK], BF16, name="q_grouped", align_bytes=64)
                 project_q(y_pixels, 0, q_grouped)
-            if step < K_BLOCKS:
+                project_without_vector(y_pixels, 3, query_weight, query_bias, q_grouped[:, :, 6:8, :])
                 quantise_k_block(k_grouped, step)
-            if projecting:
                 project_q(y_pixels, 1, q_grouped)
                 project_q(y_pixels, 2, q_grouped)
-                project_q(y_pixels, 3, q_grouped)
-            if dividing:
-                softmax_divide(step - 3, powers, total)
-                store_what_is_free(step - 3)
-            if correlating:
+            if preparing:
+                y_grouped = regroup_input(y_raw[step + 1], "y", BLOCK_PIXELS // 2)
+            if correlating and projecting:
                 correlate(step - 1)
                 windows[step - 1] = read_back(step - 1)
+            if dividing:
+                softmax_divide(step - 3, powers, total)
+            store_what_is_free(step)
             if preparing:
                 next_x_pixels = quantise_input(x_grouped, "x")
             if projecting:
@@ -337,6 +411,8 @@ def tile_local_module_pa_t_kernel(tc, x, y, query_w, query_b, key_w, key_b, out)
                     scales=q_scales[:, step * BLOCK_PIXELS : (step + 1) * BLOCK_PIXELS],
                     in_=q_grouped[:].rearrange("p j r t -> p (j r t)"),
                 )
+            if step == BLOCKS - 1:
+                quantise_k_block(k_grouped, K_BLOCKS - 1)
             if preparing:
                 next_y_pixels = quantise_input(y_grouped, "y")
             if shifting:

@@ -340,6 +340,9 @@ def tile_local_module_pa_t_kernel(tc, x, y, query_w, query_b, key_w, key_b, out)
             x_raw[block] = load_input(x, block, "x")
             y_raw[block] = load_input(y, block, "y")
 
+        warm = keep.tile([P, 1], F32)
+        nc.vector.memset(warm[:], 0.0)
+        nc.scalar.activation(out=warm[:], in_=warm[:], func=mybir.ActivationFunctionType.Exp)
         half = BLOCK_PIXELS // 2
         x_grouped = new_grouped_input("x")
         regroup_columns(nc.scalar.copy, x_raw[0], x_grouped, 0, half)
@@ -384,12 +387,15 @@ def tile_local_module_pa_t_kernel(tc, x, y, query_w, query_b, key_w, key_b, out)
                 next_y_pixels = quantise_input(y_grouped, "y")
             y_pixels = next_y_pixels
             if preparing:
-                x_grouped = regroup_input(x_raw[step + 1], "x", BLOCK_PIXELS * 3 // 4)
+                x_grouped = regroup_input(x_raw[step + 1], "x", BLOCK_PIXELS // 2)
             if projecting:
                 q_grouped = stage.tile([P, WIDTH, BLOCK_ROWS, PACK], BF16, name="q_grouped", align_bytes=64)
                 project_q(y_pixels, 0, q_grouped)
                 project_without_vector(y_pixels, 3, query_weight, query_bias, q_grouped[:, :, 6:8, :])
                 quantise_k_block(k_grouped, step)
+            if preparing:
+                next_x_pixels = quantise_input(x_grouped, "x")
+            if projecting:
                 project_q(y_pixels, 1, q_grouped)
                 project_q(y_pixels, 2, q_grouped)
             if preparing:
@@ -400,8 +406,6 @@ def tile_local_module_pa_t_kernel(tc, x, y, query_w, query_b, key_w, key_b, out)
             if dividing:
                 softmax_divide(step - 3, powers, total)
             store_what_is_free(step)
-            if preparing:
-                next_x_pixels = quantise_input(x_grouped, "x")
             if projecting:
                 k_grouped = new_k_block(step + 1)
                 project_k(x_pixels, 2, k_grouped)

@@ -198,17 +198,36 @@ def tile_local_module_pa_t_kernel(tc, x, y, query_w, query_b, key_w, key_b, out)
                 op=mybir.AluOpType.add,
             )
 
-        def project_without_vector(pixels, pair, weight, bias, target):
-            bank = multiply(pixels, pair, weight)
-            planes = stage.tile([P, PACK, WIDTH, 2], BF16, name="planes")
-            for t in range(PACK):
-                nc.scalar.activation(
-                    out=planes[:, t],
-                    in_=bank[:, t, :].rearrange("p (i j) -> p j i", i=2),
-                    func=mybir.ActivationFunctionType.Identity,
-                    bias=bias[:, t : t + 1],
-                )
-            nc.scalar.copy(out=target, in_=planes[:].rearrange("p t j i -> p j i t"))
+        def project_q_half_without_vector(pixels, grouped):
+            codes, scales = pixels
+            w_codes, w_scales = query_weight
+            rows = BLOCK_ROWS // 2
+            half = rows * WIDTH
+            planes = stage.tile([P, PACK, WIDTH, rows], BF16, name="planes")
+            for first in range(0, PACK, 2):
+                bank = project_psum.tile([P, 2, half], F32, name="bank")
+                for i in range(2):
+                    channels = slice((first + i) * P, (first + i + 1) * P)
+                    nc.tensor.matmul_mx(
+                        out=bank[:, i, :],
+                        lhsT=w_codes[:, channels].bitcast(FP8X4),
+                        lhsT_scale=w_scales[:, channels],
+                        rhs=codes[:, half:].bitcast(FP8X4),
+                        rhs_scale=scales[:, half:],
+                        start=True,
+                        stop=True,
+                    )
+                for i in range(2):
+                    nc.scalar.activation(
+                        out=planes[:, first + i],
+                        in_=bank[:, i, :].rearrange("p (i j) -> p j i", i=rows),
+                        func=mybir.ActivationFunctionType.Identity,
+                        bias=query_bias[:, first + i : first + i + 1],
+                    )
+            nc.scalar.copy(
+                out=grouped[:, :, rows:, :].rearrange("p j i t -> p j t i"),
+                in_=planes[:].rearrange("p t j i -> p j t i"),
+            )
 
         def new_k_block(k_block):
             if k_block == 0:
@@ -231,21 +250,26 @@ def tile_local_module_pa_t_kernel(tc, x, y, query_w, query_b, key_w, key_b, out)
         def correlate(block):
             last = block == BLOCKS - 1
             products = stage.tile([P, PATCHES, WINDOW_ROWS * WINDOW_COLS], F32, name="products")
+            banks = []
             for patch in range(PATCHES):
+                banks.append(corr_psum.tile([P, 2, STREAM_COLS * BLOCK_ROWS], F32, name="corr_bank"))
+            order = [(patch, half) for patch in range(PATCHES) for half in range(2)]
+            if last:
+                order = [(patch, half) for half in range(2) for patch in range(PATCHES)]
+            for patch, half in order:
                 q_cols = slice(block * BLOCK_PIXELS + patch * P, block * BLOCK_PIXELS + (patch + 1) * P)
-                bank = corr_psum.tile([P, 2, STREAM_COLS * BLOCK_ROWS], F32, name="corr_bank")
-                for half in range(2):
-                    first = (block + half) * K_BLOCK_WORDS + patch * PATCH_COLS * BLOCK_ROWS
-                    k_cols = slice(first, first + STREAM_COLS * BLOCK_ROWS)
-                    nc.tensor.matmul_mx(
-                        out=bank[:, half, :],
-                        lhsT=q_codes[:, q_cols].bitcast(FP8X4),
-                        lhsT_scale=q_scales[:, q_cols],
-                        rhs=k_codes[:, k_cols].bitcast(FP8X4),
-                        rhs_scale=k_scales[:, k_cols],
-                        start=True,
-                        stop=True,
-                    )
+                first = (block + half) * K_BLOCK_WORDS + patch * PATCH_COLS * BLOCK_ROWS
+                k_cols = slice(first, first + STREAM_COLS * BLOCK_ROWS)
+                nc.tensor.matmul_mx(
+                    out=banks[patch][:, half, :],
+                    lhsT=q_codes[:, q_cols].bitcast(FP8X4),
+                    lhsT_scale=q_scales[:, q_cols],
+                    rhs=k_codes[:, k_cols].bitcast(FP8X4),
+                    rhs_scale=k_scales[:, k_cols],
+                    start=True,
+                    stop=True,
+                )
+            for patch, bank in enumerate(banks):
                 target = products[:, patch, :].rearrange("p (h r c) -> p h r c", h=2, r=BLOCK_ROWS)
                 source = bank[:].rearrange("p h (c r) -> p h r c", r=BLOCK_ROWS)[
                     :, :, :, STREAM_SKIP : STREAM_SKIP + WINDOW_COLS
@@ -359,9 +383,7 @@ def tile_local_module_pa_t_kernel(tc, x, y, query_w, query_b, key_w, key_b, out)
         query_grouped = new_grouped_weight()
         for m in range(PACK):
             gather_weight(nc.scalar.copy, query_banks, m, query_grouped)
-        y_grouped = new_grouped_input("y")
-        y_share = BLOCK_PIXELS * 3 // 4
-        regroup_columns(nc.scalar.copy, y_raw[0], y_grouped, 0, y_share)
+        y_grouped = regroup_input(y_raw[0], "y", half)
 
         k_grouped = new_k_block(0)
         windows = {}
@@ -375,41 +397,43 @@ def tile_local_module_pa_t_kernel(tc, x, y, query_w, query_b, key_w, key_b, out)
             x_pixels = next_x_pixels
             if correlating and not projecting:
                 correlate(step - 1)
+                windows[step - 2] = read_back(step - 2)
                 windows[step - 1] = read_back(step - 1)
             if dividing:
                 powers, total = softmax_powers(windows[step - 3], shift[step - 3])
             if projecting:
                 project_k(x_pixels, 0, k_grouped)
-                project_k(x_pixels, 1, k_grouped)
             if step == 0:
                 query_weight = quantise_weight(query_grouped, "query_w")
-                regroup_columns(nc.vector.tensor_copy, y_raw[0], y_grouped, y_share, BLOCK_PIXELS)
                 next_y_pixels = quantise_input(y_grouped, "y")
             y_pixels = next_y_pixels
+            if projecting:
+                project_k(x_pixels, 1, k_grouped)
             if preparing:
                 x_grouped = regroup_input(x_raw[step + 1], "x", BLOCK_PIXELS // 2)
             if projecting:
                 q_grouped = stage.tile([P, WIDTH, BLOCK_ROWS, PACK], BF16, name="q_grouped", align_bytes=64)
                 project_q(y_pixels, 0, q_grouped)
-                project_without_vector(y_pixels, 3, query_weight, query_bias, q_grouped[:, :, 6:8, :])
+                project_q_half_without_vector(y_pixels, q_grouped)
                 quantise_k_block(k_grouped, step)
             if preparing:
                 next_x_pixels = quantise_input(x_grouped, "x")
             if projecting:
                 project_q(y_pixels, 1, q_grouped)
-                project_q(y_pixels, 2, q_grouped)
             if preparing:
-                y_grouped = regroup_input(y_raw[step + 1], "y", BLOCK_PIXELS // 2)
-            if correlating and projecting:
-                correlate(step - 1)
-                windows[step - 1] = read_back(step - 1)
-            if dividing:
-                softmax_divide(step - 3, powers, total)
-            store_what_is_free(step)
+                y_grouped = regroup_input(y_raw[step + 1], "y", BLOCK_PIXELS // 4)
             if projecting:
                 k_grouped = new_k_block(step + 1)
                 project_k(x_pixels, 2, k_grouped)
                 project_k(x_pixels, 3, k_grouped)
+            if correlating and projecting:
+                correlate(step - 1)
+                if preparing:
+                    windows[step - 1] = read_back(step - 1)
+            if dividing:
+                softmax_divide(step - 3, powers, total)
+            store_what_is_free(step)
+            if projecting:
                 nc.vector.quantize_mx(
                     out=q_codes[:, step * BLOCK_PIXELS : (step + 1) * BLOCK_PIXELS].bitcast(FP8X4),
                     scales=q_scales[:, step * BLOCK_PIXELS : (step + 1) * BLOCK_PIXELS],

@@ -66,6 +66,7 @@ def tile_local_module_pa_t_kernel(tc, x, y, query_w, query_b, key_w, key_b, out)
         weight_stage = ctx.enter_context(tc.tile_pool(name="weight_stage", bufs=2))
         raw_pool = ctx.enter_context(tc.tile_pool(name="raw", bufs=BLOCKS))
         stage = ctx.enter_context(tc.tile_pool(name="stage", bufs=2))
+        window_pool = ctx.enter_context(tc.tile_pool(name="windows", bufs=4))
         regrouped = ctx.enter_context(tc.tile_pool(name="regrouped", bufs=1))
         k_stage = ctx.enter_context(tc.tile_pool(name="k_stage", bufs=3))
         small = ctx.enter_context(tc.tile_pool(name="small", bufs=2))
@@ -90,7 +91,7 @@ def tile_local_module_pa_t_kernel(tc, x, y, query_w, query_b, key_w, key_b, out)
 
         k_first = keep.tile([P, WIDTH, BLOCK_ROWS, PACK], BF16, align_bytes=64)
         k_last = keep.tile([P, WIDTH, BLOCK_ROWS, PACK], BF16, align_bytes=64)
-        nc.vector.memset(k_first[:, :, 0:REACH, :], 0.0)
+        nc.gpsimd.memset(k_first[:, :, 0:REACH, :], 0.0)
         nc.gpsimd.memset(k_last[:, :, REACH:, :], 0.0)
 
         def load_weight(w):
@@ -157,10 +158,10 @@ def tile_local_module_pa_t_kernel(tc, x, y, query_w, query_b, key_w, key_b, out)
                     in_=raw[:, :, first:end].rearrange("p j (c i) -> p c j i", i=4),
                 )
 
-        def regroup_input(raw, name, share):
+        def regroup_input(copy, raw, name, share):
             grouped = new_grouped_input(name)
             regroup_columns(gpsimd_copy, raw, grouped, share, BLOCK_PIXELS)
-            regroup_columns(nc.scalar.copy, raw, grouped, 0, share)
+            regroup_columns(copy, raw, grouped, 0, share)
             return grouped
 
         def quantise_input(grouped, name):
@@ -291,10 +292,10 @@ def tile_local_module_pa_t_kernel(tc, x, y, query_w, query_b, key_w, key_b, out)
                     out=parked, in_=products[r:P:BLOCK_ROWS, :, r * WINDOW_COLS : r * WINDOW_COLS + PARK_RUN]
                 )
 
-        def read_back(block):
-            windows = stage.tile([P, PAIRS, PARK_STEP], F32, name="windows")
+        def read_back(block, queue=nc.sync):
+            windows = window_pool.tile([P, PAIRS, PARK_STEP], F32, name="windows")
             base = park_base(block)
-            nc.sync.dma_start(
+            queue.dma_start(
                 out=windows[:].rearrange("p m s -> p (m s)")[:, 0:PARK_READ],
                 in_=out_flat[base : base + PARK_BLOCK].rearrange("(p s) -> p s", p=P)[:, 0:PARK_READ],
             )
@@ -331,7 +332,12 @@ def tile_local_module_pa_t_kernel(tc, x, y, query_w, query_b, key_w, key_b, out)
             inverse = small.tile([P, PAIRS], F32, name="inverse")
             nc.vector.reciprocal(out=inverse[:], in_=total[:])
             for m in range(PAIRS):
-                nc.scalar.mul(out=result[:, block, m, :], in_=powers[:, m, :], mul=inverse[:, m : m + 1])
+                if block >= BLOCKS - 2 and m % 2 == 1:
+                    nc.vector.tensor_scalar_mul(
+                        out=result[:, block, m, :], in0=powers[:, m, :], scalar1=inverse[:, m : m + 1]
+                    )
+                else:
+                    nc.scalar.mul(out=result[:, block, m, :], in_=powers[:, m, :], mul=inverse[:, m : m + 1])
 
         def store(block):
             nc.sync.dma_start(
@@ -343,7 +349,7 @@ def tile_local_module_pa_t_kernel(tc, x, y, query_w, query_b, key_w, key_b, out)
 
         def store_what_is_free(step):
             for done in range(BLOCKS):
-                if max(done + 3, last_block_parked_on(done) + 2) == step:
+                if max(done + 4, last_block_parked_on(done) + 2) == step:
                     store(done)
 
         def project_k(pixels, pair, grouped):
@@ -356,8 +362,8 @@ def tile_local_module_pa_t_kernel(tc, x, y, query_w, query_b, key_w, key_b, out)
         ctx.enter_context(tc.manual_schedule())
         key_bias = load_bias(key_b, "key_bias")
         query_bias = load_bias(query_b, "query_bias")
-        x_raw = {0: load_input(x, 0, "x")}
         key_rows = load_weight(key_w)
+        x_raw = {0: load_input(x, 0, "x")}
         query_rows = load_weight(query_w)
         y_raw = {0: load_input(y, 0, "y")}
         for block in range(1, BLOCKS):
@@ -367,40 +373,41 @@ def tile_local_module_pa_t_kernel(tc, x, y, query_w, query_b, key_w, key_b, out)
         warm = keep.tile([P, 1], F32)
         nc.vector.memset(warm[:], 0.0)
         nc.scalar.activation(out=warm[:], in_=warm[:], func=mybir.ActivationFunctionType.Exp)
-        half = BLOCK_PIXELS // 2
-        x_grouped = new_grouped_input("x")
-        regroup_columns(nc.scalar.copy, x_raw[0], x_grouped, 0, half)
-        regroup_columns(nc.vector.tensor_copy, x_raw[0], x_grouped, half, BLOCK_PIXELS)
         key_banks = turn_weight(key_rows)
         key_grouped = new_grouped_weight()
         gather_weight(nc.vector.tensor_copy, key_banks, 0, key_grouped)
         gather_weight(nc.vector.tensor_copy, key_banks, 1, key_grouped)
         gather_weight(nc.scalar.copy, key_banks, 2, key_grouped)
         gather_weight(nc.scalar.copy, key_banks, 3, key_grouped)
-        next_x_pixels = quantise_input(x_grouped, "x")
         key_weight = quantise_weight(key_grouped, "key_w")
+        x_grouped = new_grouped_input("x")
+        scalar_share = BLOCK_PIXELS * 3 // 8
+        regroup_columns(nc.scalar.copy, x_raw[0], x_grouped, 0, scalar_share)
+        regroup_columns(nc.vector.tensor_copy, x_raw[0], x_grouped, scalar_share, BLOCK_PIXELS)
+        next_x_pixels = quantise_input(x_grouped, "x")
         query_banks = turn_weight(query_rows)
         query_grouped = new_grouped_weight()
-        for m in range(PACK):
-            gather_weight(nc.scalar.copy, query_banks, m, query_grouped)
-        y_grouped = regroup_input(y_raw[0], "y", half)
+        gather_weight(nc.vector.tensor_copy, query_banks, 0, query_grouped)
+        gather_weight(nc.vector.tensor_copy, query_banks, 1, query_grouped)
+        gather_weight(nc.scalar.copy, query_banks, 2, query_grouped)
+        gather_weight(nc.scalar.copy, query_banks, 3, query_grouped)
+        y_grouped = regroup_input(nc.scalar.copy, y_raw[0], "y", BLOCK_PIXELS // 2)
 
         k_grouped = new_k_block(0)
         windows = {}
         shift = {}
-        for step in range(BLOCKS + 3):
+        for step in range(BLOCKS + 4):
             projecting = step < BLOCKS
             preparing = step + 1 < BLOCKS
             correlating = 0 <= step - 1 < BLOCKS
-            shifting = 0 <= step - 2 < BLOCKS
-            dividing = 0 <= step - 3
+            shifting = 0 <= step - 3 < BLOCKS
+            dividing = 0 <= step - 4
             x_pixels = next_x_pixels
             if correlating and not projecting:
                 correlate(step - 1)
-                windows[step - 2] = read_back(step - 2)
                 windows[step - 1] = read_back(step - 1)
             if dividing:
-                powers, total = softmax_powers(windows[step - 3], shift[step - 3])
+                powers, total = softmax_powers(windows[step - 4], shift[step - 4])
             if projecting:
                 project_k(x_pixels, 0, k_grouped)
             if step == 0:
@@ -409,29 +416,33 @@ def tile_local_module_pa_t_kernel(tc, x, y, query_w, query_b, key_w, key_b, out)
             y_pixels = next_y_pixels
             if projecting:
                 project_k(x_pixels, 1, k_grouped)
+            if step == 0:
+                quantise_k_block(k_grouped, step)
             if preparing:
-                x_grouped = regroup_input(x_raw[step + 1], "x", BLOCK_PIXELS // 2)
+                x_grouped = regroup_input(nc.scalar.copy, x_raw[step + 1], "x", BLOCK_PIXELS // 2)
             if projecting:
                 q_grouped = stage.tile([P, WIDTH, BLOCK_ROWS, PACK], BF16, name="q_grouped", align_bytes=64)
                 project_q(y_pixels, 0, q_grouped)
                 project_q_half_without_vector(y_pixels, q_grouped)
+            if preparing:
+                y_grouped = regroup_input(nc.vector.tensor_copy, y_raw[step + 1], "y", BLOCK_PIXELS // 4)
+            if 0 < step < BLOCKS:
                 quantise_k_block(k_grouped, step)
             if preparing:
                 next_x_pixels = quantise_input(x_grouped, "x")
             if projecting:
                 project_q(y_pixels, 1, q_grouped)
-            if preparing:
-                y_grouped = regroup_input(y_raw[step + 1], "y", BLOCK_PIXELS // 4)
             if projecting:
                 k_grouped = new_k_block(step + 1)
                 project_k(x_pixels, 2, k_grouped)
                 project_k(x_pixels, 3, k_grouped)
             if correlating and projecting:
                 correlate(step - 1)
-                if preparing:
-                    windows[step - 1] = read_back(step - 1)
+                windows[step - 1] = read_back(step - 1, nc.sync if preparing else nc.gpsimd)
+            if shifting and not projecting:
+                shift[step - 3] = softmax_shift(windows[step - 3])
             if dividing:
-                softmax_divide(step - 3, powers, total)
+                softmax_divide(step - 4, powers, total)
             store_what_is_free(step)
             if projecting:
                 nc.vector.quantize_mx(
@@ -443,5 +454,5 @@ def tile_local_module_pa_t_kernel(tc, x, y, query_w, query_b, key_w, key_b, out)
                 quantise_k_block(k_grouped, K_BLOCKS - 1)
             if preparing:
                 next_y_pixels = quantise_input(y_grouped, "y")
-            if shifting:
-                shift[step - 2] = softmax_shift(windows[step - 2])
+            if shifting and projecting:
+                shift[step - 3] = softmax_shift(windows[step - 3])

@@ -199,36 +199,17 @@ def tile_local_module_pa_t_kernel(tc, x, y, query_w, query_b, key_w, key_b, out)
                 op=mybir.AluOpType.add,
             )
 
-        def project_q_half_without_vector(pixels, grouped):
-            codes, scales = pixels
-            w_codes, w_scales = query_weight
-            rows = BLOCK_ROWS // 2
-            half = rows * WIDTH
-            planes = stage.tile([P, PACK, WIDTH, rows], BF16, name="planes")
-            for first in range(0, PACK, 2):
-                bank = project_psum.tile([P, 2, half], F32, name="bank")
-                for i in range(2):
-                    channels = slice((first + i) * P, (first + i + 1) * P)
-                    nc.tensor.matmul_mx(
-                        out=bank[:, i, :],
-                        lhsT=w_codes[:, channels].bitcast(FP8X4),
-                        lhsT_scale=w_scales[:, channels],
-                        rhs=codes[:, half:].bitcast(FP8X4),
-                        rhs_scale=scales[:, half:],
-                        start=True,
-                        stop=True,
-                    )
-                for i in range(2):
-                    nc.scalar.activation(
-                        out=planes[:, first + i],
-                        in_=bank[:, i, :].rearrange("p (i j) -> p j i", i=rows),
-                        func=mybir.ActivationFunctionType.Identity,
-                        bias=query_bias[:, first + i : first + i + 1],
-                    )
-            nc.scalar.copy(
-                out=grouped[:, :, rows:, :].rearrange("p j i t -> p j t i"),
-                in_=planes[:].rearrange("p t j i -> p j t i"),
-            )
+        def project_without_vector(pixels, pair, weight, bias, target):
+            bank = multiply(pixels, pair, weight)
+            planes = stage.tile([P, PACK, WIDTH, 2], BF16, name="planes")
+            for t in range(PACK):
+                nc.scalar.activation(
+                    out=planes[:, t],
+                    in_=bank[:, t, :].rearrange("p (i j) -> p j i", i=2),
+                    func=mybir.ActivationFunctionType.Identity,
+                    bias=bias[:, t : t + 1],
+                )
+            nc.scalar.copy(out=target, in_=planes[:].rearrange("p t j i -> p j i t"))
 
         def new_k_block(k_block):
             if k_block == 0:
@@ -292,10 +273,10 @@ def tile_local_module_pa_t_kernel(tc, x, y, query_w, query_b, key_w, key_b, out)
                     out=parked, in_=products[r:P:BLOCK_ROWS, :, r * WINDOW_COLS : r * WINDOW_COLS + PARK_RUN]
                 )
 
-        def read_back(block, queue=nc.sync):
+        def read_back(block):
             windows = window_pool.tile([P, PAIRS, PARK_STEP], F32, name="windows")
             base = park_base(block)
-            queue.dma_start(
+            nc.sync.dma_start(
                 out=windows[:].rearrange("p m s -> p (m s)")[:, 0:PARK_READ],
                 in_=out_flat[base : base + PARK_BLOCK].rearrange("(p s) -> p s", p=P)[:, 0:PARK_READ],
             )
@@ -405,6 +386,7 @@ def tile_local_module_pa_t_kernel(tc, x, y, query_w, query_b, key_w, key_b, out)
             x_pixels = next_x_pixels
             if correlating and not projecting:
                 correlate(step - 1)
+                windows[step - 2] = read_back(step - 2)
                 windows[step - 1] = read_back(step - 1)
             if dividing:
                 powers, total = softmax_powers(windows[step - 4], shift[step - 4])
@@ -423,22 +405,24 @@ def tile_local_module_pa_t_kernel(tc, x, y, query_w, query_b, key_w, key_b, out)
             if projecting:
                 q_grouped = stage.tile([P, WIDTH, BLOCK_ROWS, PACK], BF16, name="q_grouped", align_bytes=64)
                 project_q(y_pixels, 0, q_grouped)
-                project_q_half_without_vector(y_pixels, q_grouped)
+                project_without_vector(y_pixels, 3, query_weight, query_bias, q_grouped[:, :, 6:8, :])
             if preparing:
-                y_grouped = regroup_input(nc.vector.tensor_copy, y_raw[step + 1], "y", BLOCK_PIXELS // 4)
+                y_grouped = regroup_input(nc.scalar.copy, y_raw[step + 1], "y", BLOCK_PIXELS // 2)
             if 0 < step < BLOCKS:
                 quantise_k_block(k_grouped, step)
             if preparing:
                 next_x_pixels = quantise_input(x_grouped, "x")
             if projecting:
                 project_q(y_pixels, 1, q_grouped)
+                project_q(y_pixels, 2, q_grouped)
             if projecting:
                 k_grouped = new_k_block(step + 1)
                 project_k(x_pixels, 2, k_grouped)
                 project_k(x_pixels, 3, k_grouped)
             if correlating and projecting:
                 correlate(step - 1)
-                windows[step - 1] = read_back(step - 1, nc.sync if preparing else nc.gpsimd)
+                if preparing:
+                    windows[step - 1] = read_back(step - 1)
             if shifting and not projecting:
                 shift[step - 3] = softmax_shift(windows[step - 3])
             if dividing:

from contextlib import ExitStack

import concourse.mybir as mybir
from concourse.masks import make_identity

F32 = mybir.dt.float32
BF16 = mybir.dt.bfloat16
U32 = mybir.dt.uint32
U8 = mybir.dt.uint8
I32 = mybir.dt.int32
FP8X4 = mybir.dt.float8_e4m3fn_x4

P = 128
PACK = 4
CHANNELS = P * PACK
HEIGHT = 64
WIDTH = 64
REACH = 4
SHIFTS = 2 * REACH + 1
CELLS = SHIFTS * SHIFTS

BLOCK_ROWS = 8
BLOCKS = HEIGHT // BLOCK_ROWS
BLOCK_PIXELS = BLOCK_ROWS * WIDTH
PAIR_PIXELS = 2 * WIDTH
PAIRS = BLOCK_ROWS // 2

PATCH_COLS = P // BLOCK_ROWS
PATCHES = WIDTH // PATCH_COLS
WINDOW_ROWS = BLOCK_ROWS + 2 * REACH
WINDOW_COLS = PATCH_COLS + 2 * REACH
K_BLOCKS = BLOCKS + 1
K_MARGIN = 8
K_COLS = WIDTH + 2 * K_MARGIN
K_BLOCK_WORDS = K_COLS * BLOCK_ROWS
STREAM_COLS = 32
STREAM_SKIP = K_MARGIN - REACH

PARK_RUN = SHIFTS * WINDOW_COLS
PARK_STEP = PARK_RUN + 1
PARK_READ = (PAIRS - 1) * PARK_STEP + (SHIFTS - 1) * WINDOW_COLS + SHIFTS
PARK_ROW = WIDTH * PARK_STEP
PARK_BLOCK = BLOCK_ROWS * PARK_ROW
PARK_SLOTS = 2
OUT_FLOATS = HEIGHT * WIDTH * CELLS
OUT_BLOCK = BLOCK_PIXELS * CELLS
PARK_START = OUT_FLOATS - PARK_SLOTS * PARK_BLOCK

FLOPS = 2 * 2 * CHANNELS * CHANNELS * HEIGHT * WIDTH + 2 * CHANNELS * CELLS * HEIGHT * WIDTH


def park_base(block):
    return PARK_START + (block % PARK_SLOTS) * PARK_BLOCK


def last_block_parked_on(block):
    first, end = block * OUT_BLOCK, (block + 1) * OUT_BLOCK
    users = [b for b in range(BLOCKS) if park_base(b) < end and first < park_base(b) + PARK_BLOCK]
    return max(users) if users else -1


def tile_local_module_pa_t_kernel(tc, x, y, query_w, query_b, key_w, key_b, out):
    nc = tc.nc
    with ExitStack() as ctx:
        keep = ctx.enter_context(tc.tile_pool(name="keep", bufs=1))
        weight_stage = ctx.enter_context(tc.tile_pool(name="weight_stage", bufs=2))
        raw_pool = ctx.enter_context(tc.tile_pool(name="raw", bufs=BLOCKS))
        stage = ctx.enter_context(tc.tile_pool(name="stage", bufs=2))
        window_pool = ctx.enter_context(tc.tile_pool(name="windows", bufs=4))
        regrouped = ctx.enter_context(tc.tile_pool(name="regrouped", bufs=1))
        k_stage = ctx.enter_context(tc.tile_pool(name="k_stage", bufs=3))
        small = ctx.enter_context(tc.tile_pool(name="small", bufs=2))
        project_psum = ctx.enter_context(tc.psum_pool(name="project_psum", bufs=4))
        corr_psum = ctx.enter_context(tc.psum_pool(name="corr_psum", bufs=4))

        q_codes = keep.tile([P, BLOCKS * BLOCK_PIXELS], U32, align_bytes=64)
        q_scales = keep.tile([P, BLOCKS * BLOCK_PIXELS], U8, align_bytes=64)
        k_codes = keep.tile([P, K_BLOCKS * K_BLOCK_WORDS], U32, align_bytes=64)
        k_scales = keep.tile([P, K_BLOCKS * K_BLOCK_WORDS], U8, align_bytes=64)
        result = keep.tile([P, BLOCKS, PAIRS, CELLS], F32)
        identity = keep.tile([P, P], F32)
        make_identity(nc, identity[:])

        margin_words = K_MARGIN * BLOCK_ROWS
        code_blocks = k_codes[:].bitcast(I32).rearrange("p (b w) -> p b w", w=K_BLOCK_WORDS)
        scale_blocks = k_scales[:].bitcast(I32).rearrange("p (b w) -> p b w", w=K_BLOCK_WORDS // 4)
        nc.vector.memset(code_blocks[:, :, 0:margin_words], 0)
        nc.vector.memset(code_blocks[:, :, K_BLOCK_WORDS - margin_words :], 0)
        nc.vector.memset(scale_blocks[:, :, 0 : margin_words // 4], 0)
        nc.vector.memset(scale_blocks[:, :, (K_BLOCK_WORDS - margin_words) // 4 :], 0)

        k_first = keep.tile([P, WIDTH, BLOCK_ROWS, PACK], BF16, align_bytes=64)
        k_last = keep.tile([P, WIDTH, BLOCK_ROWS, PACK], BF16, align_bytes=64)
        nc.gpsimd.memset(k_first[:, :, 0:REACH, :], 0.0)
        nc.gpsimd.memset(k_last[:, :, REACH:, :], 0.0)

        def load_weight(w):
            rows = weight_stage.tile([P, PACK, CHANNELS], BF16, name="w_rows")
            for m in range(0, PACK, 2):
                nc.sync.dma_start(
                    out=rows[:, m : m + 2, :], in_=w.rearrange("(p m) c -> p m c", m=PACK)[:, m : m + 2, :]
                )
            return rows

        def turn_weight(rows):
            banks = []
            for m in range(PACK):
                flipped = corr_psum.tile([P, 2, P], F32, name="flipped", tag="corr_bank")
                words = rows[:, m, :].bitcast(F32)
                for u in range(2):
                    nc.tensor.transpose(flipped[:, u, :], words[:, u::2], identity[:])
                banks.append(flipped)
            return banks

        def new_grouped_weight():
            return weight_stage.tile([P, CHANNELS, PACK], BF16, name="w_grouped", align_bytes=64)

        def gather_weight(copy, banks, m, grouped):
            copy(
                out=grouped[:, m * P : (m + 1) * P, :].rearrange("p o j -> p (o j)").bitcast(F32)
                .rearrange("p (o u) -> p o u", u=2),
                in_=banks[m][:].rearrange("p u o -> p o u"),
            )

        def quantise_weight(grouped, name):
            codes = keep.tile([P, CHANNELS], U32, name=name + "_codes", align_bytes=64)
            scales = keep.tile([P, CHANNELS], U8, name=name + "_scales", align_bytes=64)
            nc.vector.quantize_mx(
                out=codes[:].bitcast(FP8X4), scales=scales[:], in_=grouped[:].rearrange("p o j -> p (o j)")
            )
            return codes, scales

        def load_bias(b, name):
            bias = keep.tile([P, PACK], BF16, name=name)
            nc.scalar.dma_start(out=bias[:], in_=b.rearrange("(p t) -> p t", t=PACK))
            return bias

        def load_input(image, block, name):
            planes = image.rearrange("b (p j) h w -> p (b j) (h w)", j=PACK)
            raw = raw_pool.tile([P, PACK, BLOCK_PIXELS], BF16, name=name + "_raw")
            nc.sync.dma_start(out=raw[:], in_=planes[:, :, block * BLOCK_PIXELS : (block + 1) * BLOCK_PIXELS])
            return raw

        def new_grouped_input(name):
            return regrouped.tile([P, BLOCK_PIXELS, PACK], BF16, name=name + "_grouped", align_bytes=64)

        def gpsimd_copy(out, in_):
            nc.gpsimd.tensor_scalar(
                out=out, in0=in_, scalar1=1.0, scalar2=0.0, op0=mybir.AluOpType.mult, op1=mybir.AluOpType.add
            )

        def regroup_columns(copy, raw, grouped, first, end):
            if copy is gpsimd_copy:
                copy(out=grouped[:, first:end, :], in_=raw[:, :, first:end].rearrange("p j c -> p c j"))
            else:
                copy(
                    out=grouped[:, first:end, :].rearrange("p (c i) j -> p c j i", i=4),
                    in_=raw[:, :, first:end].rearrange("p j (c i) -> p c j i", i=4),
                )

        def regroup_input(copy, raw, name, share):
            grouped = new_grouped_input(name)
            regroup_columns(gpsimd_copy, raw, grouped, share, BLOCK_PIXELS)
            regroup_columns(copy, raw, grouped, 0, share)
            return grouped

        def quantise_input(grouped, name):
            codes = stage.tile([P, BLOCK_PIXELS], U32, name=name + "_codes", align_bytes=64)
            scales = stage.tile([P, BLOCK_PIXELS], U8, name=name + "_scales", align_bytes=64)
            nc.vector.quantize_mx(
                out=codes[:].bitcast(FP8X4), scales=scales[:], in_=grouped[:].rearrange("p w j -> p (w j)")
            )
            return codes, scales

        def multiply(pixels, pair, weight):
            codes, scales = pixels
            w_codes, w_scales = weight
            cols = slice(pair * PAIR_PIXELS, (pair + 1) * PAIR_PIXELS)
            bank = project_psum.tile([P, PACK, PAIR_PIXELS], F32, name="bank")
            for t in range(PACK):
                channels = slice(t * P, (t + 1) * P)
                nc.tensor.matmul_mx(
                    out=bank[:, t, :],
                    lhsT=w_codes[:, channels].bitcast(FP8X4),
                    lhsT_scale=w_scales[:, channels],
                    rhs=codes[:, cols].bitcast(FP8X4),
                    rhs_scale=scales[:, cols],
                    start=True,
                    stop=True,
                )
            return bank

        def project(pixels, pair, weight, bias, target):
            bank = multiply(pixels, pair, weight)
            nc.vector.tensor_tensor(
                out=target,
                in0=bank[:].rearrange("p t (i j) -> p j i t", i=2),
                in1=bias[:].unsqueeze(1).unsqueeze(1).to_broadcast([P, WIDTH, 2, PACK]),
                op=mybir.AluOpType.add,
            )

        def project_without_vector(pixels, pair, weight, bias, target):
            bank = multiply(pixels, pair, weight)
            planes = stage.tile([P, PACK, WIDTH, 2], BF16, name="planes")
            for t in range(PACK):
                nc.scalar.activation(
                    out=planes[:, t],
                    in_=bank[:, t, :].rearrange("p (i j) -> p j i", i=2),
                    func=mybir.ActivationFunctionType.Identity,
                    bias=bias[:, t : t + 1],
                )
            nc.scalar.copy(out=target, in_=planes[:].rearrange("p t j i -> p j i t"))

        def new_k_block(k_block):
            if k_block == 0:
                return k_first
            if k_block == K_BLOCKS - 1:
                return k_last
            return k_stage.tile([P, WIDTH, BLOCK_ROWS, PACK], BF16, name="k_grouped", align_bytes=64)

        def quantise_k_block(grouped, k_block):
            first = k_block * K_BLOCK_WORDS + margin_words
            nc.vector.quantize_mx(
                out=k_codes[:, first : first + BLOCK_PIXELS].bitcast(FP8X4),
                scales=k_scales[:, first : first + BLOCK_PIXELS],
                in_=grouped[:].rearrange("p j r t -> p (j r t)"),
            )

        out_flat = out.rearrange("b h w d -> (b h w d)")
        out_pixels = out.rearrange("b h w d -> (b h w) d")

        def correlate(block):
            last = block == BLOCKS - 1
            products = stage.tile([P, PATCHES, WINDOW_ROWS * WINDOW_COLS], F32, name="products")
            banks = []
            for patch in range(PATCHES):
                banks.append(corr_psum.tile([P, 2, STREAM_COLS * BLOCK_ROWS], F32, name="corr_bank"))
            order = [(patch, half) for patch in range(PATCHES) for half in range(2)]
            if last:
                order = [(patch, half) for half in range(2) for patch in range(PATCHES)]
            for patch, half in order:
                q_cols = slice(block * BLOCK_PIXELS + patch * P, block * BLOCK_PIXELS + (patch + 1) * P)
                first = (block + half) * K_BLOCK_WORDS + patch * PATCH_COLS * BLOCK_ROWS
                k_cols = slice(first, first + STREAM_COLS * BLOCK_ROWS)
                nc.tensor.matmul_mx(
                    out=banks[patch][:, half, :],
                    lhsT=q_codes[:, q_cols].bitcast(FP8X4),
                    lhsT_scale=q_scales[:, q_cols],
                    rhs=k_codes[:, k_cols].bitcast(FP8X4),
                    rhs_scale=k_scales[:, k_cols],
                    start=True,
                    stop=True,
                )
            for patch, bank in enumerate(banks):
                target = products[:, patch, :].rearrange("p (h r c) -> p h r c", h=2, r=BLOCK_ROWS)
                source = bank[:].rearrange("p h (c r) -> p h r c", r=BLOCK_ROWS)[
                    :, :, :, STREAM_SKIP : STREAM_SKIP + WINDOW_COLS
                ]
                if last and patch % 2 == 1:
                    nc.vector.tensor_scalar_mul(out=target, in0=source, scalar1=1.0 / CHANNELS)
                else:
                    nc.scalar.mul(out=target, in_=source, mul=1.0 / CHANNELS)
            half_rows = BLOCK_ROWS // 2
            for turn in range(BLOCK_ROWS):
                r = turn // 2 + turn % 2 * half_rows
                row_base = park_base(block) + r * PARK_ROW
                parked = (
                    out_flat[row_base : row_base + PARK_ROW]
                    .rearrange("(a s) -> a s", s=PATCH_COLS * PARK_STEP)[:, 0 : PATCH_COLS * PARK_RUN]
                    .rearrange("a (c s) -> c a s", s=PARK_RUN)
                )
                nc.sync.dma_start(
                    out=parked, in_=products[r:P:BLOCK_ROWS, :, r * WINDOW_COLS : r * WINDOW_COLS + PARK_RUN]
                )

        def read_back(block):
            windows = window_pool.tile([P, PAIRS, PARK_STEP], F32, name="windows")
            base = park_base(block)
            nc.sync.dma_start(
                out=windows[:].rearrange("p m s -> p (m s)")[:, 0:PARK_READ],
                in_=out_flat[base : base + PARK_BLOCK].rearrange("(p s) -> p s", p=P)[:, 0:PARK_READ],
            )
            return windows

        def window_cells(windows):
            return windows[:, :, 0:PARK_RUN].rearrange("p m (d c) -> p m d c", c=WINDOW_COLS)[:, :, :, 0:SHIFTS]

        def softmax_shift(windows):
            shift = small.tile([P, PAIRS], F32, name="shift")
            nc.vector.tensor_reduce(
                out=shift[:],
                in_=window_cells(windows),
                axis=mybir.AxisListType.XY,
                op=mybir.AluOpType.max,
                negate=True,
            )
            return shift

        def softmax_powers(windows, shift):
            powers = stage.tile([P, PAIRS, CELLS], F32, name="powers")
            total = small.tile([P, PAIRS], F32, name="total")
            for m in range(PAIRS):
                nc.scalar.activation(
                    out=powers[:, m, :].rearrange("p (d c) -> p d c", c=SHIFTS),
                    in_=window_cells(windows)[:, m],
                    func=mybir.ActivationFunctionType.Exp,
                    bias=shift[:, m : m + 1],
                    accum_out=total[:, m : m + 1],
                )
            return powers, total

        def softmax_divide(block, powers, total):
            inverse = small.tile([P, PAIRS], F32, name="inverse")
            nc.vector.reciprocal(out=inverse[:], in_=total[:])
            for m in range(PAIRS):
                if block >= BLOCKS - 2 and m % 2 == 1:
                    nc.vector.tensor_scalar_mul(
                        out=result[:, block, m, :], in0=powers[:, m, :], scalar1=inverse[:, m : m + 1]
                    )
                else:
                    nc.scalar.mul(out=result[:, block, m, :], in_=powers[:, m, :], mul=inverse[:, m : m + 1])

        def store(block):
            nc.sync.dma_start(
                out=out_pixels[block * BLOCK_PIXELS : (block + 1) * BLOCK_PIXELS, :].rearrange(
                    "(p m) d -> p (m d)", p=P
                ),
                in_=result[:, block].rearrange("p m d -> p (m d)"),
            )

        def store_what_is_free(step):
            for done in range(BLOCKS):
                if max(done + 4, last_block_parked_on(done) + 2) == step:
                    store(done)

        def project_k(pixels, pair, grouped):
            first = (2 * pair + REACH) % BLOCK_ROWS
            project(pixels, pair, key_weight, key_bias, grouped[:, :, first : first + 2, :])

        def project_q(pixels, pair, grouped):
            project(pixels, pair, query_weight, query_bias, grouped[:, :, 2 * pair : 2 * pair + 2, :])

        ctx.enter_context(tc.manual_schedule())
        key_bias = load_bias(key_b, "key_bias")
        query_bias = load_bias(query_b, "query_bias")
        key_rows = load_weight(key_w)
        x_raw = {0: load_input(x, 0, "x")}
        query_rows = load_weight(query_w)
        y_raw = {0: load_input(y, 0, "y")}
        for block in range(1, BLOCKS):
            x_raw[block] = load_input(x, block, "x")
            y_raw[block] = load_input(y, block, "y")

        warm = keep.tile([P, 1], F32)
        nc.vector.memset(warm[:], 0.0)
        nc.scalar.activation(out=warm[:], in_=warm[:], func=mybir.ActivationFunctionType.Exp)
        key_banks = turn_weight(key_rows)
        key_grouped = new_grouped_weight()
        gather_weight(nc.vector.tensor_copy, key_banks, 0, key_grouped)
        gather_weight(nc.vector.tensor_copy, key_banks, 1, key_grouped)
        gather_weight(nc.scalar.copy, key_banks, 2, key_grouped)
        gather_weight(nc.scalar.copy, key_banks, 3, key_grouped)
        key_weight = quantise_weight(key_grouped, "key_w")
        x_grouped = new_grouped_input("x")
        scalar_share = BLOCK_PIXELS * 3 // 8
        regroup_columns(nc.scalar.copy, x_raw[0], x_grouped, 0, scalar_share)
        regroup_columns(nc.vector.tensor_copy, x_raw[0], x_grouped, scalar_share, BLOCK_PIXELS)
        next_x_pixels = quantise_input(x_grouped, "x")
        query_banks = turn_weight(query_rows)
        query_grouped = new_grouped_weight()
        gather_weight(nc.vector.tensor_copy, query_banks, 0, query_grouped)
        gather_weight(nc.vector.tensor_copy, query_banks, 1, query_grouped)
        gather_weight(nc.scalar.copy, query_banks, 2, query_grouped)
        gather_weight(nc.scalar.copy, query_banks, 3, query_grouped)
        y_grouped = regroup_input(nc.scalar.copy, y_raw[0], "y", BLOCK_PIXELS // 2)

        k_grouped = new_k_block(0)
        windows = {}
        shift = {}
        for step in range(BLOCKS + 4):
            projecting = step < BLOCKS
            preparing = step + 1 < BLOCKS
            correlating = 0 <= step - 1 < BLOCKS
            shifting = 0 <= step - 3 < BLOCKS
            dividing = 0 <= step - 4
            x_pixels = next_x_pixels
            if correlating and not projecting:
                correlate(step - 1)
                windows[step - 2] = read_back(step - 2)
                windows[step - 1] = read_back(step - 1)
            if dividing:
                powers, total = softmax_powers(windows[step - 4], shift[step - 4])
            if projecting:
                project_k(x_pixels, 0, k_grouped)
            if step == 0:
                query_weight = quantise_weight(query_grouped, "query_w")
                next_y_pixels = quantise_input(y_grouped, "y")
            y_pixels = next_y_pixels
            if projecting:
                project_k(x_pixels, 1, k_grouped)
            if step == 0:
                quantise_k_block(k_grouped, step)
            if preparing:
                x_grouped = regroup_input(nc.scalar.copy, x_raw[step + 1], "x", BLOCK_PIXELS // 2)
            if projecting:
                q_grouped = stage.tile([P, WIDTH, BLOCK_ROWS, PACK], BF16, name="q_grouped", align_bytes=64)
                project_q(y_pixels, 0, q_grouped)
                project_without_vector(y_pixels, 3, query_weight, query_bias, q_grouped[:, :, 6:8, :])
            if preparing:
                y_grouped = regroup_input(nc.scalar.copy, y_raw[step + 1], "y", BLOCK_PIXELS // 2)
            if 0 < step < BLOCKS:
                quantise_k_block(k_grouped, step)
            if preparing:
                next_x_pixels = quantise_input(x_grouped, "x")
            if projecting:
                project_q(y_pixels, 1, q_grouped)
                project_q(y_pixels, 2, q_grouped)
            if projecting:
                k_grouped = new_k_block(step + 1)
                project_k(x_pixels, 2, k_grouped)
                project_k(x_pixels, 3, k_grouped)
            if correlating and projecting:
                correlate(step - 1)
                if preparing:
                    windows[step - 1] = read_back(step - 1)
            if shifting and not projecting:
                shift[step - 3] = softmax_shift(windows[step - 3])
            if dividing:
                softmax_divide(step - 4, powers, total)
            store_what_is_free(step)
            if projecting:
                nc.vector.quantize_mx(
                    out=q_codes[:, step * BLOCK_PIXELS : (step + 1) * BLOCK_PIXELS].bitcast(FP8X4),
                    scales=q_scales[:, step * BLOCK_PIXELS : (step + 1) * BLOCK_PIXELS],
                    in_=q_grouped[:].rearrange("p j r t -> p (j r t)"),
                )
            if step == BLOCKS - 1:
                quantise_k_block(k_grouped, K_BLOCKS - 1)
            if preparing:
                next_y_pixels = quantise_input(y_grouped, "y")
            if shifting and projecting:
                shift[step - 3] = softmax_shift(windows[step - 3])
